import numpy as np
import ml_dtypes

BF16 = ml_dtypes.bfloat16


def bf(x):
    return np.asarray(x, np.float32).astype(BF16)


def f32(x):
    return np.asarray(x, np.float32)


def f64(x):
    return np.asarray(x).astype(np.float64)


def striped(idx):
    return np.tile(idx.reshape(-1, 16).T, (8, 1))


C, V, B, T, N = 256, 512, 4, 64, 256


def pos_encoding():
    t = np.arange(T, dtype=np.float64)[None, :]
    c = np.arange(C, dtype=np.float64)[:, None]
    ang = t / np.power(10000.0, 2.0 * (c // 2) / C)
    return np.where((np.arange(C) % 2 == 0)[:, None], np.sin(ang), np.cos(ang))


def setup_inputs():
    return {"emb": f32(0.1 * np.random.standard_normal((C, V))), "pos": f32(np.tile(pos_encoding(), (1, B))), "offs": striped(np.random.permutation(np.tile(np.arange(V), 2))[:N])}


def reference(emb, pos, offs):
    idx = offs[:16].T.reshape(-1)
    scaled = f64(emb) * np.sqrt(C)
    return scaled[:, idx] + f64(pos)

@@ -1,0 +1,35 @@
+import concourse.mybir as mybir
+
+F32 = mybir.dt.float32
+U16 = mybir.dt.uint16
+ADD = mybir.AluOpType.add
+
+P = 128
+C, V, N = 256, 512, 256
+SCALE = 16.0
+
+
+def tile_texttransformer_kernel(tc, emb, pos, offs, out):
+    nc = tc.nc
+    with (
+        tc.tile_pool(name="held", bufs=1) as held,
+        tc.tile_pool(name="work", bufs=2) as work,
+    ):
+        offsets = held.tile([P, N // 16], U16, name="offsets")
+        nc.sync.dma_start(offsets[:], offs)
+
+        for block in range(C // P):
+            rows = slice(block * P, (block + 1) * P)
+
+            table = work.tile([P, V], F32)
+            nc.sync.dma_start(table[:], emb[rows, :])
+            places = work.tile([P, N], F32)
+            nc.scalar.dma_start(places[:], pos[rows, :])
+
+            scaled = work.tile([P, V], F32)
+            nc.vector.tensor_scalar_mul(scaled[:], table[:], SCALE)
+
+            summed = work.tile([P, N], F32)
+            nc.vector.tensor_tensor(summed[:], scaled[:].indirect(offsets[:]), places[:], ADD)
+
+            nc.sync.dma_start(out[rows, :], summed[:])

@@ -18,13 +18,16 @@ def tile_texttransformer_kernel(tc, emb, pos, offs, out):
         offsets = held.tile([P, N // 16], U16, name="offsets")
         nc.sync.dma_start(offsets[:], offs)
 
+        queues = (nc.sync, nc.scalar)
+
         for block in range(C // P):
             rows = slice(block * P, (block + 1) * P)
+            queue = queues[block % 2]
 
             table = work.tile([P, V], F32)
-            nc.sync.dma_start(table[:], emb[rows, :])
+            queue.dma_start(table[:], emb[rows, :])
             places = work.tile([P, N], F32)
-            nc.scalar.dma_start(places[:], pos[rows, :])
+            nc.gpsimd.dma_start(places[:], pos[rows, :])
 
             scaled = work.tile([P, V], F32)
             nc.vector.tensor_scalar_mul(scaled[:], table[:], SCALE)
@@ -32,4 +35,4 @@ def tile_texttransformer_kernel(tc, emb, pos, offs, out):
             summed = work.tile([P, N], F32)
             nc.vector.tensor_tensor(summed[:], scaled[:].indirect(offsets[:]), places[:], ADD)
 
-            nc.sync.dma_start(out[rows, :], summed[:])
+            queue.dma_start(out[rows, :], summed[:])

@@ -18,21 +18,21 @@ def tile_texttransformer_kernel(tc, emb, pos, offs, out):
         offsets = held.tile([P, N // 16], U16, name="offsets")
         nc.sync.dma_start(offsets[:], offs)
 
-        queues = (nc.sync, nc.scalar)
-
         for block in range(C // P):
             rows = slice(block * P, (block + 1) * P)
-            queue = queues[block % 2]
 
             table = work.tile([P, V], F32)
-            queue.dma_start(table[:], emb[rows, :])
+            nc.scalar.dma_start(table[:], emb[rows, :])
             places = work.tile([P, N], F32)
-            nc.gpsimd.dma_start(places[:], pos[rows, :])
+            nc.sync.dma_start(places[:], pos[rows, :])
 
             scaled = work.tile([P, V], F32)
-            nc.vector.tensor_scalar_mul(scaled[:], table[:], SCALE)
+            if block % 2 == 0:
+                nc.vector.tensor_scalar_mul(scaled[:], table[:], SCALE)
+            else:
+                nc.scalar.mul(scaled[:], table[:], SCALE)
 
             summed = work.tile([P, N], F32)
             nc.vector.tensor_tensor(summed[:], scaled[:].indirect(offsets[:]), places[:], ADD)
 
-            queue.dma_start(out[rows, :], summed[:])
+            nc.sync.dma_start(out[rows, :], summed[:])

@@ -22,17 +22,14 @@ def tile_texttransformer_kernel(tc, emb, pos, offs, out):
             rows = slice(block * P, (block + 1) * P)
 
             table = work.tile([P, V], F32)
-            nc.scalar.dma_start(table[:], emb[rows, :])
+            nc.sync.dma_start(table[:], emb[rows, :])
             places = work.tile([P, N], F32)
             nc.sync.dma_start(places[:], pos[rows, :])
 
             scaled = work.tile([P, V], F32)
-            if block % 2 == 0:
-                nc.vector.tensor_scalar_mul(scaled[:], table[:], SCALE)
-            else:
-                nc.scalar.mul(scaled[:], table[:], SCALE)
+            nc.vector.tensor_scalar_mul(scaled[:], table[:], SCALE)
 
             summed = work.tile([P, N], F32)
             nc.vector.tensor_tensor(summed[:], scaled[:].indirect(offsets[:]), places[:], ADD)
 
-            nc.sync.dma_start(out[rows, :], summed[:])
+            nc.scalar.dma_start(out[rows, :], summed[:])

@@ -7,29 +7,36 @@ ADD = mybir.AluOpType.add
 P = 128
 C, V, N = 256, 512, 256
 SCALE = 16.0
+BLOCKS = C // P
 
 
 def tile_texttransformer_kernel(tc, emb, pos, offs, out):
     nc = tc.nc
     with (
         tc.tile_pool(name="held", bufs=1) as held,
-        tc.tile_pool(name="work", bufs=2) as work,
+        tc.tile_pool(name="work", bufs=BLOCKS) as work,
     ):
         offsets = held.tile([P, N // 16], U16, name="offsets")
         nc.sync.dma_start(offsets[:], offs)
 
-        for block in range(C // P):
-            rows = slice(block * P, (block + 1) * P)
-
+        tables = []
+        for block in range(BLOCKS):
             table = work.tile([P, V], F32)
-            nc.sync.dma_start(table[:], emb[rows, :])
+            nc.sync.dma_start(table[:], emb[block * P : (block + 1) * P, :])
+            tables.append(table)
+        places_of = []
+        for block in range(BLOCKS):
             places = work.tile([P, N], F32)
-            nc.sync.dma_start(places[:], pos[rows, :])
+            nc.sync.dma_start(places[:], pos[block * P : (block + 1) * P, :])
+            places_of.append(places)
 
+        windows = []
+        for block in range(BLOCKS):
             scaled = work.tile([P, V], F32)
-            nc.vector.tensor_scalar_mul(scaled[:], table[:], SCALE)
+            nc.vector.tensor_scalar_mul(scaled[:], tables[block][:], SCALE)
+            windows.append(scaled)
 
+        for block in range(BLOCKS):
             summed = work.tile([P, N], F32)
-            nc.vector.tensor_tensor(summed[:], scaled[:].indirect(offsets[:]), places[:], ADD)
-
-            nc.scalar.dma_start(out[rows, :], summed[:])
+            nc.vector.tensor_tensor(summed[:], windows[block][:].indirect(offsets[:]), places_of[block][:], ADD)
+            nc.scalar.dma_start(out[block * P : (block + 1) * P, :], summed[:])

@@ -16,14 +16,15 @@ def tile_texttransformer_kernel(tc, emb, pos, offs, out):
         tc.tile_pool(name="held", bufs=1) as held,
         tc.tile_pool(name="work", bufs=BLOCKS) as work,
     ):
-        offsets = held.tile([P, N // 16], U16, name="offsets")
-        nc.sync.dma_start(offsets[:], offs)
-
         tables = []
         for block in range(BLOCKS):
             table = work.tile([P, V], F32)
             nc.sync.dma_start(table[:], emb[block * P : (block + 1) * P, :])
             tables.append(table)
+
+        offsets = held.tile([P, N // 16], U16, name="offsets")
+        nc.sync.dma_start(offsets[:], offs)
+
         places_of = []
         for block in range(BLOCKS):
             places = work.tile([P, N], F32)

@@ -23,13 +23,14 @@ def tile_texttransformer_kernel(tc, emb, pos, offs, out):
             tables.append(table)
 
         offsets = held.tile([P, N // 16], U16, name="offsets")
-        nc.sync.dma_start(offsets[:], offs)
 
         places_of = []
         for block in range(BLOCKS):
             places = work.tile([P, N], F32)
             nc.sync.dma_start(places[:], pos[block * P : (block + 1) * P, :])
             places_of.append(places)
+            if block == 0:
+                nc.sync.dma_start(offsets[:], offs)
 
         windows = []
         for block in range(BLOCKS):

@@ -8,6 +8,8 @@ P = 128
 C, V, N = 256, 512, 256
 SCALE = 16.0
 BLOCKS = C // P
+ENTRIES = 16
+PIECES = (2, 1)
 
 
 def tile_texttransformer_kernel(tc, emb, pos, offs, out):
@@ -22,15 +24,19 @@ def tile_texttransformer_kernel(tc, emb, pos, offs, out):
             nc.sync.dma_start(table[:], emb[block * P : (block + 1) * P, :])
             tables.append(table)
 
-        offsets = held.tile([P, N // 16], U16, name="offsets")
+        offsets = held.tile([P, N // ENTRIES], U16, name="offsets")
 
         places_of = []
         for block in range(BLOCKS):
             places = work.tile([P, N], F32)
-            nc.sync.dma_start(places[:], pos[block * P : (block + 1) * P, :])
+            width = N // PIECES[block]
+            for start in range(0, N, width):
+                nc.sync.dma_start(
+                    places[:, start : start + width], pos[block * P : (block + 1) * P, start : start + width]
+                )
+                if block == 0 and start == 0:
+                    nc.sync.dma_start(offsets[:], offs)
             places_of.append(places)
-            if block == 0:
-                nc.sync.dma_start(offsets[:], offs)
 
         windows = []
         for block in range(BLOCKS):
@@ -40,5 +46,13 @@ def tile_texttransformer_kernel(tc, emb, pos, offs, out):
 
         for block in range(BLOCKS):
             summed = work.tile([P, N], F32)
-            nc.vector.tensor_tensor(summed[:], windows[block][:].indirect(offsets[:]), places_of[block][:], ADD)
+            width = N // PIECES[block]
+            for start in range(0, N, width):
+                entries = offsets[:, start // ENTRIES : (start + width) // ENTRIES]
+                nc.vector.tensor_tensor(
+                    summed[:, start : start + width],
+                    windows[block][:].indirect(entries),
+                    places_of[block][:, start : start + width],
+                    ADD,
+                )
             nc.scalar.dma_start(out[block * P : (block + 1) * P, :], summed[:])

@@ -3,56 +3,49 @@ import concourse.mybir as mybir
 F32 = mybir.dt.float32
 U16 = mybir.dt.uint16
 ADD = mybir.AluOpType.add
+COPY = mybir.ActivationFunctionType.Copy
 
 P = 128
 C, V, N = 256, 512, 256
 SCALE = 16.0
-BLOCKS = C // P
 ENTRIES = 16
-PIECES = (2, 1)
+HALF = V // 2
+PIECE = N // 2
 
 
 def tile_texttransformer_kernel(tc, emb, pos, offs, out):
     nc = tc.nc
-    with (
-        tc.tile_pool(name="held", bufs=1) as held,
-        tc.tile_pool(name="work", bufs=BLOCKS) as work,
-    ):
-        tables = []
-        for block in range(BLOCKS):
-            table = work.tile([P, V], F32)
-            nc.sync.dma_start(table[:], emb[block * P : (block + 1) * P, :])
-            tables.append(table)
+    with tc.tile_pool(name="held", bufs=1) as held:
+        zeros = held.tile([P, 1], F32, name="zeros")
+        warmed = held.tile([P, 1], F32, name="warmed")
+        nc.gpsimd.memset(zeros[:], 0.0)
+        nc.scalar.activation(warmed[:], zeros[:], COPY)
 
+        table0 = held.tile([P, V], F32, name="table0")
+        table1 = held.tile([P, V], F32, name="table1")
+        places0 = held.tile([P, N], F32, name="places0")
+        places1 = held.tile([P, N], F32, name="places1")
         offsets = held.tile([P, N // ENTRIES], U16, name="offsets")
 
-        places_of = []
-        for block in range(BLOCKS):
-            places = work.tile([P, N], F32)
-            width = N // PIECES[block]
-            for start in range(0, N, width):
-                nc.sync.dma_start(
-                    places[:, start : start + width], pos[block * P : (block + 1) * P, start : start + width]
-                )
-                if block == 0 and start == 0:
-                    nc.sync.dma_start(offsets[:], offs)
-            places_of.append(places)
+        nc.sync.dma_start(table0[:], emb[0:P, :])
+        nc.sync.dma_start(places0[:, 0:PIECE], pos[0:P, 0:PIECE])
+        nc.sync.dma_start(offsets[:], offs)
+        nc.sync.dma_start(table1[:], emb[P:C, :])
+        nc.sync.dma_start(places0[:, PIECE:N], pos[0:P, PIECE:N])
+        nc.sync.dma_start(places1[:], pos[P:C, :])
 
-        windows = []
-        for block in range(BLOCKS):
-            scaled = work.tile([P, V], F32)
-            nc.vector.tensor_scalar_mul(scaled[:], tables[block][:], SCALE)
-            windows.append(scaled)
+        scaled0 = held.tile([P, V], F32, name="scaled0")
+        scaled1 = held.tile([P, V], F32, name="scaled1")
+        summed0 = held.tile([P, N], F32, name="summed0")
+        summed1 = held.tile([P, N], F32, name="summed1")
+        first, rest = offsets[:, 0 : PIECE // ENTRIES], offsets[:, PIECE // ENTRIES : N // ENTRIES]
 
-        for block in range(BLOCKS):
-            summed = work.tile([P, N], F32)
-            width = N // PIECES[block]
-            for start in range(0, N, width):
-                entries = offsets[:, start // ENTRIES : (start + width) // ENTRIES]
-                nc.vector.tensor_tensor(
-                    summed[:, start : start + width],
-                    windows[block][:].indirect(entries),
-                    places_of[block][:, start : start + width],
-                    ADD,
-                )
-            nc.scalar.dma_start(out[block * P : (block + 1) * P, :], summed[:])
+        nc.vector.tensor_scalar_mul(scaled0[:], table0[:], SCALE)
+        nc.vector.tensor_tensor(summed0[:, 0:PIECE], scaled0[:].indirect(first), places0[:, 0:PIECE], ADD)
+        nc.vector.tensor_scalar_mul(scaled1[:, 0:HALF], table1[:, 0:HALF], SCALE)
+        nc.scalar.activation(scaled1[:, HALF:V], table1[:, HALF:V], COPY, scale=SCALE)
+        nc.vector.tensor_tensor(summed0[:, PIECE:N], scaled0[:].indirect(rest), places0[:, PIECE:N], ADD)
+        nc.vector.tensor_tensor(summed1[:], scaled1[:].indirect(offsets[:]), places1[:], ADD)
+
+        nc.scalar.dma_start(out[0:P, :], summed0[:])
+        nc.scalar.dma_start(out[P:C, :], summed1[:])

@@ -3,24 +3,17 @@ import concourse.mybir as mybir
 F32 = mybir.dt.float32
 U16 = mybir.dt.uint16
 ADD = mybir.AluOpType.add
-COPY = mybir.ActivationFunctionType.Copy
 
 P = 128
 C, V, N = 256, 512, 256
 SCALE = 16.0
 ENTRIES = 16
-HALF = V // 2
 PIECE = N // 2
 
 
 def tile_texttransformer_kernel(tc, emb, pos, offs, out):
     nc = tc.nc
     with tc.tile_pool(name="held", bufs=1) as held:
-        zeros = held.tile([P, 1], F32, name="zeros")
-        warmed = held.tile([P, 1], F32, name="warmed")
-        nc.gpsimd.memset(zeros[:], 0.0)
-        nc.scalar.activation(warmed[:], zeros[:], COPY)
-
         table0 = held.tile([P, V], F32, name="table0")
         table1 = held.tile([P, V], F32, name="table1")
         places0 = held.tile([P, N], F32, name="places0")
@@ -42,8 +35,7 @@ def tile_texttransformer_kernel(tc, emb, pos, offs, out):
 
         nc.vector.tensor_scalar_mul(scaled0[:], table0[:], SCALE)
         nc.vector.tensor_tensor(summed0[:, 0:PIECE], scaled0[:].indirect(first), places0[:, 0:PIECE], ADD)
-        nc.vector.tensor_scalar_mul(scaled1[:, 0:HALF], table1[:, 0:HALF], SCALE)
-        nc.scalar.activation(scaled1[:, HALF:V], table1[:, HALF:V], COPY, scale=SCALE)
+        nc.vector.tensor_scalar_mul(scaled1[:], table1[:], SCALE)
         nc.vector.tensor_tensor(summed0[:, PIECE:N], scaled0[:].indirect(rest), places0[:, PIECE:N], ADD)
         nc.vector.tensor_tensor(summed1[:], scaled1[:].indirect(offsets[:]), places1[:], ADD)
 

import concourse.mybir as mybir

F32 = mybir.dt.float32
U16 = mybir.dt.uint16
ADD = mybir.AluOpType.add

P = 128
C, V, N = 256, 512, 256
SCALE = 16.0
ENTRIES = 16
PIECE = N // 2


def tile_texttransformer_kernel(tc, emb, pos, offs, out):
    nc = tc.nc
    with tc.tile_pool(name="held", bufs=1) as held:
        table0 = held.tile([P, V], F32, name="table0")
        table1 = held.tile([P, V], F32, name="table1")
        places0 = held.tile([P, N], F32, name="places0")
        places1 = held.tile([P, N], F32, name="places1")
        offsets = held.tile([P, N // ENTRIES], U16, name="offsets")

        nc.sync.dma_start(table0[:], emb[0:P, :])
        nc.sync.dma_start(places0[:, 0:PIECE], pos[0:P, 0:PIECE])
        nc.sync.dma_start(offsets[:], offs)
        nc.sync.dma_start(table1[:], emb[P:C, :])
        nc.sync.dma_start(places0[:, PIECE:N], pos[0:P, PIECE:N])
        nc.sync.dma_start(places1[:], pos[P:C, :])

        scaled0 = held.tile([P, V], F32, name="scaled0")
        scaled1 = held.tile([P, V], F32, name="scaled1")
        summed0 = held.tile([P, N], F32, name="summed0")
        summed1 = held.tile([P, N], F32, name="summed1")
        first, rest = offsets[:, 0 : PIECE // ENTRIES], offsets[:, PIECE // ENTRIES : N // ENTRIES]

        nc.vector.tensor_scalar_mul(scaled0[:], table0[:], SCALE)
        nc.vector.tensor_tensor(summed0[:, 0:PIECE], scaled0[:].indirect(first), places0[:, 0:PIECE], ADD)
        nc.vector.tensor_scalar_mul(scaled1[:], table1[:], SCALE)
        nc.vector.tensor_tensor(summed0[:, PIECE:N], scaled0[:].indirect(rest), places0[:, PIECE:N], ADD)
        nc.vector.tensor_tensor(summed1[:], scaled1[:].indirect(offsets[:]), places1[:], ADD)

        nc.scalar.dma_start(out[0:P, :], summed0[:])
        nc.scalar.dma_start(out[P:C, :], summed1[:])
